import numpy as np
import ml_dtypes


def mxq(x, axis, fmt="e4m3"):
    dtype, down = {"e4m3": (ml_dtypes.float8_e4m3fn, 7), "e5m2": (ml_dtypes.float8_e5m2, 14)}[fmt]
    v = np.moveaxis(np.asarray(x, np.float32).astype(ml_dtypes.bfloat16).astype(np.float64), axis, -1)
    blocks = v.reshape(v.shape[:-1] + (-1, 32))
    amax = np.abs(blocks).max(-1, keepdims=True)
    byte = np.maximum(np.where(amax > 0, np.frexp(amax)[1] - 1 + 127, 0) - down, 1)
    scale = np.exp2(byte - 127.0)
    codes = (blocks / scale).astype(np.float32).astype(dtype).astype(np.float64)
    return np.moveaxis((codes * scale).reshape(v.shape), -1, axis)


WIDE = False


def mx_kscale(k):
    if not WIDE:
        return np.ones(k)
    levels = np.array([10, -10, 5, -5, 0])
    a = np.random.permutation(np.resize(levels, k // 512 * 4)).reshape(k // 512, 4)
    idx = np.arange(k)
    return np.exp2(a[idx // 512, idx % 128 // 32])


BF16 = ml_dtypes.bfloat16


def bf(x):
    return np.asarray(x, np.float32).astype(BF16)


def f64(x):
    return np.asarray(x).astype(np.float64)


B, Tq, Tk, C = 2, 128, 512, 512
BETA = 2.35


def softplus(v):
    return np.log(1.0 + np.exp(v))


def setup_inputs():
    s = mx_kscale(C)
    level = np.random.standard_normal((B, Tk))[..., None]
    return {"q": bf(np.random.standard_normal((B, Tq, C)) * 1.5 * s),
            "k_mu": bf(np.random.standard_normal((B, Tk, C)) / s),
            "k_var": bf(softplus(np.random.standard_normal((B, Tk, C)) + level) / s / s),
            "v_sample": bf(np.random.standard_normal((B, Tk, C)) * 1.3)}


def reference(q, k_mu, k_var, v_sample):
    mean_scores = (mxq(f64(q), 2, "e4m3") @ mxq(f64(k_mu), 2, "e4m3").transpose(0, 2, 1)) / np.sqrt(C)
    q2 = f64(q) * f64(q)
    var_penalty = (mxq(q2, 2, "e4m3") @ mxq(f64(k_var), 2, "e4m3").transpose(0, 2, 1)) / C
    scores = mean_scores - BETA * np.sqrt(var_penalty)
    e = np.exp(scores - scores.max(-1, keepdims=True))
    return (mxq(e, 2, "e4m3") @ mxq(f64(v_sample), 1, "e4m3")) / e.sum(-1, keepdims=True)

@@ -1,0 +1,176 @@
+import math
+from contextlib import ExitStack
+
+import concourse.mybir as mybir
+from concourse.masks import make_identity
+
+BF16 = mybir.dt.bfloat16
+F32 = mybir.dt.float32
+U32 = mybir.dt.uint32
+U8 = mybir.dt.uint8
+FP8X4 = mybir.dt.float8_e4m3fn_x4
+ACT = mybir.ActivationFunctionType
+ALU = mybir.AluOpType
+AX = mybir.AxisListType
+
+B, TQ, TK, C = 2, 128, 512, 512
+BETA = 2.35
+P = 128
+PACK = 4
+FLOPS = 3 * 2 * B * TQ * TK * C
+
+
+def load_four_rows_a_partition(nc, pool, rows, name):
+    raw = pool.tile([P, PACK * C], BF16, name=name)
+    nc.sync.dma_start(out=raw[:], in_=rows.rearrange("(p j) c -> p (j c)", j=PACK))
+    return raw
+
+
+def channels_to_partitions(nc, psum_tr, ident_f32, raw, grouped, copies):
+    groups = raw.shape[1] // C
+    words = raw[:].bitcast(F32).rearrange("p (j u w) -> p j u w", j=groups, u=2)
+    grouped_words = grouped[:].bitcast(F32).rearrange(
+        "p (h j r u) -> p h j r u", h=groups // 2, j=2, u=2
+    )
+    for h in range(groups // 2):
+        bank = psum_tr.tile([P, 2, 2, P], F32, name="bank", tag="bank")
+        for j in range(2):
+            for u in range(2):
+                nc.tensor.transpose(bank[:, j, u, :], words[:, 2 * h + j, u, :], ident_f32[:])
+        copies[h](out=grouped_words[:, h], in_=bank[:].rearrange("p j u r -> p j r u"))
+
+
+def quantise(nc, pool, grouped, name):
+    columns = grouped.shape[1] // PACK
+    codes = pool.tile([P, columns], U32, name=name + "_codes", align_bytes=64)
+    scales = pool.tile([P, columns], U8, name=name + "_scales", align_bytes=64)
+    nc.vector.quantize_mx(out=codes[:].bitcast(FP8X4), scales=scales[:], in_=grouped[:])
+    return codes, scales
+
+
+def mx_pass(nc, acc, stationary, moving):
+    nc.tensor.matmul_mx(
+        out=acc,
+        lhsT=stationary[0].bitcast(FP8X4),
+        lhsT_scale=stationary[1],
+        rhs=moving[0].bitcast(FP8X4),
+        rhs_scale=moving[1],
+        start=True,
+        stop=True,
+    )
+
+
+def tile_probcrossattention_pb_s_kernel(tc, q, k_mu, k_var, v_sample, out):
+    nc = tc.nc
+    with ExitStack() as ctx:
+        keep = ctx.enter_context(tc.tile_pool(name="keep", bufs=1))
+        psum_tr = ctx.enter_context(tc.psum_pool(name="psum_tr", bufs=4))
+        psum_acc = ctx.enter_context(tc.psum_pool(name="psum_acc", bufs=3))
+        psum_et = ctx.enter_context(tc.psum_pool(name="psum_et", bufs=1))
+
+        q_raw = keep.tile([P, B * C], BF16, name="q_raw")
+        nc.sync.dma_start(
+            out=q_raw[:].rearrange("p (b c) -> p b c", b=B), in_=q.rearrange("b q c -> q b c")
+        )
+        var_raw = [load_four_rows_a_partition(nc, keep, k_var[b], "var_raw%d" % b) for b in range(B)]
+        mu_raw = [load_four_rows_a_partition(nc, keep, k_mu[b], "mu_raw%d" % b) for b in range(B)]
+        v_raw = [load_four_rows_a_partition(nc, keep, v_sample[b], "v_raw%d" % b) for b in range(B)]
+
+        ident_f32 = keep.tile([P, P], F32, name="ident_f32")
+        make_identity(nc, ident_f32[:])
+        ident_bf16 = keep.tile([P, P], BF16, name="ident_bf16")
+        make_identity(nc, ident_bf16[:])
+        one = keep.tile([P, 1], F32, name="one")
+        nc.vector.memset(one[:], 1.0)
+        warm_sqrt = keep.tile([P, 1], F32, name="warm_sqrt")
+        nc.scalar.activation(out=warm_sqrt[:], in_=one[:], func=ACT.Sqrt)
+
+        q_grouped = keep.tile([P, B * TQ * PACK], BF16, name="q_grouped", align_bytes=64)
+        channels_to_partitions(nc, psum_tr, ident_f32, q_raw, q_grouped, [nc.vector.tensor_copy])
+        q2_grouped = keep.tile([P, B * TQ * PACK], BF16, name="q2_grouped", align_bytes=64)
+        nc.vector.tensor_tensor(out=q2_grouped[:], in0=q_grouped[:], in1=q_grouped[:], op=ALU.mult)
+        q_mx = quantise(nc, keep, q_grouped, "q")
+        q2_mx = quantise(nc, keep, q2_grouped, "q2")
+
+        def queries(mx, b):
+            return (mx[0][:, b * TQ : (b + 1) * TQ], mx[1][:, b * TQ : (b + 1) * TQ])
+
+        def whole(mx):
+            return (mx[0][:], mx[1][:])
+
+        penalty = []
+        for b in range(B):
+            var_grouped = keep.tile([P, TK * PACK], BF16, name="var_grouped%d" % b, align_bytes=64)
+            channels_to_partitions(
+                nc, psum_tr, ident_f32, var_raw[b], var_grouped, [nc.scalar.copy, nc.vector.tensor_copy]
+            )
+            var_mx = quantise(nc, keep, var_grouped, "var%d" % b)
+            var_acc = psum_acc.tile([P, TK], F32, name="var_acc", tag="acc")
+            mx_pass(nc, var_acc[:], queries(q2_mx, b), whole(var_mx))
+            pen = keep.tile([P, TK], F32, name="penalty%d" % b)
+            nc.scalar.activation(out=pen[:], in_=var_acc[:], func=ACT.Sqrt, scale=BETA * BETA / C)
+            penalty.append(pen)
+        warm_exp = keep.tile([P, 1], F32, name="warm_exp")
+        nc.scalar.activation(out=warm_exp[:], in_=penalty[B - 1][:, 0:1], func=ACT.Exp, scale=0.0)
+
+        e_rows = []
+        inv_sum = []
+        for b in range(B):
+            mu_grouped = keep.tile([P, TK * PACK], BF16, name="mu_grouped%d" % b, align_bytes=64)
+            channels_to_partitions(
+                nc, psum_tr, ident_f32, mu_raw[b], mu_grouped, [nc.scalar.copy, nc.scalar.copy]
+            )
+            mu_mx = quantise(nc, keep, mu_grouped, "mu%d" % b)
+            mean_acc = psum_acc.tile([P, TK], F32, name="mean_acc", tag="acc")
+            mx_pass(nc, mean_acc[:], queries(q_mx, b), whole(mu_mx))
+            neg_scores = keep.tile([P, TK], F32, name="neg_scores%d" % b)
+            nc.vector.scalar_tensor_tensor(
+                out=neg_scores[:],
+                in0=mean_acc[:],
+                scalar=-1.0 / math.sqrt(C),
+                in1=penalty[b][:],
+                op0=ALU.mult,
+                op1=ALU.add,
+            )
+            neg_max = keep.tile([P, 1], F32, name="neg_max%d" % b)
+            nc.vector.tensor_reduce(out=neg_max[:], in_=neg_scores[:], axis=AX.X, op=ALU.min)
+            e_bf16 = keep.tile([P, TK], BF16, name="e_bf16_%d" % b)
+            row_sum = keep.tile([P, 1], F32, name="row_sum%d" % b)
+            nc.scalar.activation(
+                out=e_bf16[:],
+                in_=neg_scores[:],
+                func=ACT.Exp,
+                bias=neg_max[:],
+                scale=-1.0,
+                accum_out=row_sum[:],
+            )
+            inv = keep.tile([P, 1], F32, name="inv_sum%d" % b)
+            nc.vector.reciprocal(out=inv[:], in_=row_sum[:])
+            e_rows.append(e_bf16)
+            inv_sum.append(inv)
+
+        v_mx = []
+        regroup = [nc.scalar.copy, nc.vector.tensor_copy]
+        for b in range(B):
+            v_grouped = keep.tile([P, C * PACK], BF16, name="v_grouped%d" % b, align_bytes=64)
+            regroup[b](
+                out=v_grouped[:].rearrange("p (c i t) -> p c t i", i=4, t=PACK),
+                in_=v_raw[b][:].rearrange("p (t c i) -> p c t i", t=PACK, i=4),
+            )
+            v_mx.append(quantise(nc, keep, v_grouped, "v%d" % b))
+
+        for b in range(B):
+            e_t = psum_et.tile([P, PACK, TQ], BF16, name="e_t", tag="e_t")
+            for t in range(PACK):
+                nc.tensor.transpose(e_t[:, t, :], e_rows[b][:, t * P : (t + 1) * P], ident_bf16[:])
+            e_grouped = keep.tile([P, TQ * PACK], BF16, name="e_grouped%d" % b, align_bytes=64)
+            nc.scalar.copy(
+                out=e_grouped[:].rearrange("p (r t) -> p r t", t=PACK),
+                in_=e_t[:].rearrange("p t r -> p r t"),
+            )
+            e_mx = quantise(nc, keep, e_grouped, "e%d" % b)
+            out_acc = psum_acc.tile([P, C], F32, name="out_acc", tag="acc")
+            mx_pass(nc, out_acc[:], whole(e_mx), whole(v_mx[b]))
+            out_sb = keep.tile([P, C], F32, name="out_sb%d" % b)
+            nc.scalar.activation(out=out_sb[:], in_=out_acc[:], func=ACT.Copy, scale=inv_sum[b][:])
+            nc.sync.dma_start(out=out[b], in_=out_sb[:])

@@ -19,33 +19,15 @@ P = 128
 PACK = 4
 FLOPS = 3 * 2 * B * TQ * TK * C
 
-
-def load_four_rows_a_partition(nc, pool, rows, name):
-    raw = pool.tile([P, PACK * C], BF16, name=name)
-    nc.sync.dma_start(out=raw[:], in_=rows.rearrange("(p j) c -> p (j c)", j=PACK))
-    return raw
+K_ORDER = (("var", 0), ("mu", 0), ("var", 1), ("mu", 1))
+HALF_KEYS = TK // 2
+LAG = 4
 
 
-def channels_to_partitions(nc, psum_tr, ident_f32, raw, grouped, copies):
-    groups = raw.shape[1] // C
-    words = raw[:].bitcast(F32).rearrange("p (j u w) -> p j u w", j=groups, u=2)
-    grouped_words = grouped[:].bitcast(F32).rearrange(
-        "p (h j r u) -> p h j r u", h=groups // 2, j=2, u=2
-    )
-    for h in range(groups // 2):
-        bank = psum_tr.tile([P, 2, 2, P], F32, name="bank", tag="bank")
-        for j in range(2):
-            for u in range(2):
-                nc.tensor.transpose(bank[:, j, u, :], words[:, 2 * h + j, u, :], ident_f32[:])
-        copies[h](out=grouped_words[:, h], in_=bank[:].rearrange("p j u r -> p j r u"))
-
-
-def quantise(nc, pool, grouped, name):
-    columns = grouped.shape[1] // PACK
-    codes = pool.tile([P, columns], U32, name=name + "_codes", align_bytes=64)
-    scales = pool.tile([P, columns], U8, name=name + "_scales", align_bytes=64)
-    nc.vector.quantize_mx(out=codes[:].bitcast(FP8X4), scales=scales[:], in_=grouped[:])
-    return codes, scales
+def words_to_partitions(nc, bank, rows, ident_f32):
+    for g in range(2):
+        for u in range(2):
+            nc.tensor.transpose(bank[:, g, u, :], rows[:, g, u, :], ident_f32[:])
 
 
 def mx_pass(nc, acc, stationary, moving):
@@ -65,16 +47,30 @@ def tile_probcrossattention_pb_s_kernel(tc, q, k_mu, k_var, v_sample, out):
     with ExitStack() as ctx:
         keep = ctx.enter_context(tc.tile_pool(name="keep", bufs=1))
         psum_tr = ctx.enter_context(tc.psum_pool(name="psum_tr", bufs=4))
-        psum_acc = ctx.enter_context(tc.psum_pool(name="psum_acc", bufs=3))
-        psum_et = ctx.enter_context(tc.psum_pool(name="psum_et", bufs=1))
+        psum_acc = ctx.enter_context(tc.psum_pool(name="psum_acc", bufs=4))
+        ctx.enter_context(tc.manual_schedule())
+
+        halves = [(kind, b, h) for (kind, b) in K_ORDER for h in range(2)]
+        k_dram = {"var": k_var, "mu": k_mu}
 
         q_raw = keep.tile([P, B * C], BF16, name="q_raw")
         nc.sync.dma_start(
             out=q_raw[:].rearrange("p (b c) -> p b c", b=B), in_=q.rearrange("b q c -> q b c")
         )
-        var_raw = [load_four_rows_a_partition(nc, keep, k_var[b], "var_raw%d" % b) for b in range(B)]
-        mu_raw = [load_four_rows_a_partition(nc, keep, k_mu[b], "mu_raw%d" % b) for b in range(B)]
-        v_raw = [load_four_rows_a_partition(nc, keep, v_sample[b], "v_raw%d" % b) for b in range(B)]
+        k_raw = {}
+        for kind, b in K_ORDER:
+            k_raw[(kind, b)] = keep.tile([P, PACK * C], BF16, name="%s_raw%d" % (kind, b))
+        for kind, b, h in halves:
+            cols = slice(h * 2 * C, (h + 1) * 2 * C)
+            nc.sync.dma_start(
+                out=k_raw[(kind, b)][:, cols],
+                in_=k_dram[kind][b].rearrange("(p j) c -> p (j c)", j=PACK)[:, cols],
+            )
+        v_raw = []
+        for b in range(B):
+            raw = keep.tile([P, PACK * C], BF16, name="v_raw%d" % b)
+            nc.sync.dma_start(out=raw[:], in_=v_sample[b].rearrange("(p j) c -> p (j c)", j=PACK))
+            v_raw.append(raw)
 
         ident_f32 = keep.tile([P, P], F32, name="ident_f32")
         make_identity(nc, ident_f32[:])
@@ -85,92 +81,138 @@ def tile_probcrossattention_pb_s_kernel(tc, q, k_mu, k_var, v_sample, out):
         warm_sqrt = keep.tile([P, 1], F32, name="warm_sqrt")
         nc.scalar.activation(out=warm_sqrt[:], in_=one[:], func=ACT.Sqrt)
 
+        q_bank = psum_tr.tile([P, B, 2, P], F32, name="q_bank", tag="bank")
+        words_to_partitions(
+            nc, q_bank, q_raw[:].bitcast(F32).rearrange("p (b u w) -> p b u w", b=B, u=2), ident_f32
+        )
         q_grouped = keep.tile([P, B * TQ * PACK], BF16, name="q_grouped", align_bytes=64)
-        channels_to_partitions(nc, psum_tr, ident_f32, q_raw, q_grouped, [nc.vector.tensor_copy])
+        nc.scalar.copy(
+            out=q_grouped[:].bitcast(F32).rearrange("p (b r u) -> p b r u", b=B, u=2),
+            in_=q_bank[:].rearrange("p b u r -> p b r u"),
+        )
         q2_grouped = keep.tile([P, B * TQ * PACK], BF16, name="q2_grouped", align_bytes=64)
         nc.vector.tensor_tensor(out=q2_grouped[:], in0=q_grouped[:], in1=q_grouped[:], op=ALU.mult)
-        q_mx = quantise(nc, keep, q_grouped, "q")
-        q2_mx = quantise(nc, keep, q2_grouped, "q2")
+        q_mx = {}
+        for kind, grouped in (("mu", q_grouped), ("var", q2_grouped)):
+            codes = keep.tile([P, B * TQ], U32, name="q_codes_" + kind, align_bytes=64)
+            scales = keep.tile([P, B * TQ], U8, name="q_scales_" + kind, align_bytes=64)
+            nc.vector.quantize_mx(out=codes[:].bitcast(FP8X4), scales=scales[:], in_=grouped[:])
+            q_mx[kind] = (codes, scales)
 
-        def queries(mx, b):
-            return (mx[0][:, b * TQ : (b + 1) * TQ], mx[1][:, b * TQ : (b + 1) * TQ])
+        k_grouped = {}
+        k_codes = {}
+        k_scales = {}
+        k_acc = {}
+        penalty = {}
+        neg_scores = {}
+        neg_max = {}
+        v_grouped = {}
+        for step in range(len(halves) + LAG):
+            ripe = halves[step - LAG] if step >= LAG else None
+            takes_root = ripe is not None and ripe[0] == "var" and ripe[2] == 1
+            if step < len(halves):
+                kind, b, h = halves[step]
+                x = (kind, b)
+                if h == 0:
+                    k_grouped[x] = keep.tile(
+                        [P, TK * PACK], BF16, name="%s_grouped%d" % x, align_bytes=64
+                    )
+                    k_codes[x] = keep.tile([P, TK], U32, name="%s_codes%d" % x, align_bytes=64)
+                    k_scales[x] = keep.tile([P, TK], U8, name="%s_scales%d" % x, align_bytes=64)
+                bank = psum_tr.tile([P, 2, 2, P], F32, name="bank", tag="bank")
+                words_to_partitions(
+                    nc,
+                    bank,
+                    k_raw[x][:].bitcast(F32).rearrange("p (h j u w) -> p h j u w", h=2, j=2, u=2)[:, h],
+                    ident_f32,
+                )
+                empty = nc.vector.tensor_copy if takes_root else nc.scalar.copy
+                empty(
+                    out=k_grouped[x][:].bitcast(F32).rearrange("p (h j r u) -> p h j r u", h=2, j=2, u=2)[:, h],
+                    in_=bank[:].rearrange("p j u r -> p j r u"),
+                )
+                keys = slice(h * HALF_KEYS, (h + 1) * HALF_KEYS)
+                nc.vector.quantize_mx(
+                    out=k_codes[x][:, keys].bitcast(FP8X4),
+                    scales=k_scales[x][:, keys],
+                    in_=k_grouped[x][:, h * HALF_KEYS * PACK : (h + 1) * HALF_KEYS * PACK],
+                )
+            if ripe is not None:
+                kind, b, h = ripe
+                x = (kind, b)
+                if h == 0:
+                    k_acc[x] = psum_acc.tile([P, TK], F32, name="k_acc", tag="acc")
+                keys = slice(h * HALF_KEYS, (h + 1) * HALF_KEYS)
+                queries = slice(b * TQ, (b + 1) * TQ)
+                mx_pass(
+                    nc,
+                    k_acc[x][:, keys],
+                    (q_mx[kind][0][:, queries], q_mx[kind][1][:, queries]),
+                    (k_codes[x][:, keys], k_scales[x][:, keys]),
+                )
+                if h == 1 and kind == "var":
+                    penalty[b] = keep.tile([P, TK], F32, name="penalty%d" % b)
+                    nc.scalar.activation(
+                        out=penalty[b][:], in_=k_acc[x][:], func=ACT.Sqrt, scale=BETA * BETA / C
+                    )
+                if h == 1 and kind == "mu":
+                    neg_scores[b] = keep.tile([P, TK], F32, name="neg_scores%d" % b)
+                    nc.vector.scalar_tensor_tensor(
+                        out=neg_scores[b][:],
+                        in0=k_acc[x][:],
+                        scalar=-1.0 / math.sqrt(C),
+                        in1=penalty[b][:],
+                        op0=ALU.mult,
+                        op1=ALU.add,
+                    )
+                    neg_max[b] = keep.tile([P, 1], F32, name="neg_max%d" % b)
+                    nc.vector.tensor_reduce(out=neg_max[b][:], in_=neg_scores[b][:], axis=AX.X, op=ALU.min)
+                    v_grouped[b] = keep.tile([P, C * PACK], BF16, name="v_grouped%d" % b, align_bytes=64)
+                    nc.vector.tensor_copy(
+                        out=v_grouped[b][:].rearrange("p (c i t) -> p c t i", i=4, t=PACK),
+                        in_=v_raw[b][:].rearrange("p (t c i) -> p c t i", t=PACK, i=4),
+                    )
 
-        def whole(mx):
-            return (mx[0][:], mx[1][:])
-
-        penalty = []
-        for b in range(B):
-            var_grouped = keep.tile([P, TK * PACK], BF16, name="var_grouped%d" % b, align_bytes=64)
-            channels_to_partitions(
-                nc, psum_tr, ident_f32, var_raw[b], var_grouped, [nc.scalar.copy, nc.vector.tensor_copy]
-            )
-            var_mx = quantise(nc, keep, var_grouped, "var%d" % b)
-            var_acc = psum_acc.tile([P, TK], F32, name="var_acc", tag="acc")
-            mx_pass(nc, var_acc[:], queries(q2_mx, b), whole(var_mx))
-            pen = keep.tile([P, TK], F32, name="penalty%d" % b)
-            nc.scalar.activation(out=pen[:], in_=var_acc[:], func=ACT.Sqrt, scale=BETA * BETA / C)
-            penalty.append(pen)
         warm_exp = keep.tile([P, 1], F32, name="warm_exp")
-        nc.scalar.activation(out=warm_exp[:], in_=penalty[B - 1][:, 0:1], func=ACT.Exp, scale=0.0)
-
-        e_rows = []
-        inv_sum = []
+        nc.scalar.activation(out=warm_exp[:], in_=one[:], func=ACT.Exp)
+        row_sum = {}
+        e_t = {}
         for b in range(B):
-            mu_grouped = keep.tile([P, TK * PACK], BF16, name="mu_grouped%d" % b, align_bytes=64)
-            channels_to_partitions(
-                nc, psum_tr, ident_f32, mu_raw[b], mu_grouped, [nc.scalar.copy, nc.scalar.copy]
-            )
-            mu_mx = quantise(nc, keep, mu_grouped, "mu%d" % b)
-            mean_acc = psum_acc.tile([P, TK], F32, name="mean_acc", tag="acc")
-            mx_pass(nc, mean_acc[:], queries(q_mx, b), whole(mu_mx))
-            neg_scores = keep.tile([P, TK], F32, name="neg_scores%d" % b)
-            nc.vector.scalar_tensor_tensor(
-                out=neg_scores[:],
-                in0=mean_acc[:],
-                scalar=-1.0 / math.sqrt(C),
-                in1=penalty[b][:],
-                op0=ALU.mult,
-                op1=ALU.add,
-            )
-            neg_max = keep.tile([P, 1], F32, name="neg_max%d" % b)
-            nc.vector.tensor_reduce(out=neg_max[:], in_=neg_scores[:], axis=AX.X, op=ALU.min)
             e_bf16 = keep.tile([P, TK], BF16, name="e_bf16_%d" % b)
-            row_sum = keep.tile([P, 1], F32, name="row_sum%d" % b)
+            row_sum[b] = keep.tile([P, 1], F32, name="row_sum%d" % b)
             nc.scalar.activation(
                 out=e_bf16[:],
-                in_=neg_scores[:],
+                in_=neg_scores[b][:],
                 func=ACT.Exp,
-                bias=neg_max[:],
+                bias=neg_max[b][:],
                 scale=-1.0,
-                accum_out=row_sum[:],
+                accum_out=row_sum[b][:],
             )
-            inv = keep.tile([P, 1], F32, name="inv_sum%d" % b)
-            nc.vector.reciprocal(out=inv[:], in_=row_sum[:])
-            e_rows.append(e_bf16)
-            inv_sum.append(inv)
-
-        v_mx = []
-        regroup = [nc.scalar.copy, nc.vector.tensor_copy]
-        for b in range(B):
-            v_grouped = keep.tile([P, C * PACK], BF16, name="v_grouped%d" % b, align_bytes=64)
-            regroup[b](
-                out=v_grouped[:].rearrange("p (c i t) -> p c t i", i=4, t=PACK),
-                in_=v_raw[b][:].rearrange("p (t c i) -> p c t i", t=PACK, i=4),
-            )
-            v_mx.append(quantise(nc, keep, v_grouped, "v%d" % b))
-
-        for b in range(B):
-            e_t = psum_et.tile([P, PACK, TQ], BF16, name="e_t", tag="e_t")
+            e_t[b] = psum_tr.tile([P, PACK, TQ], BF16, name="e_t", tag="bank")
             for t in range(PACK):
-                nc.tensor.transpose(e_t[:, t, :], e_rows[b][:, t * P : (t + 1) * P], ident_bf16[:])
-            e_grouped = keep.tile([P, TQ * PACK], BF16, name="e_grouped%d" % b, align_bytes=64)
+                nc.tensor.transpose(e_t[b][:, t, :], e_bf16[:, t * P : (t + 1) * P], ident_bf16[:])
+        e_grouped = {}
+        for b in range(B):
+            e_grouped[b] = keep.tile([P, TQ * PACK], BF16, name="e_grouped%d" % b, align_bytes=64)
             nc.scalar.copy(
-                out=e_grouped[:].rearrange("p (r t) -> p r t", t=PACK),
-                in_=e_t[:].rearrange("p t r -> p r t"),
+                out=e_grouped[b][:].rearrange("p (r t) -> p r t", t=PACK),
+                in_=e_t[b][:].rearrange("p t r -> p r t"),
             )
-            e_mx = quantise(nc, keep, e_grouped, "e%d" % b)
+
+        for b in range(B):
+            inv_sum = keep.tile([P, 1], F32, name="inv_sum%d" % b)
+            nc.vector.reciprocal(out=inv_sum[:], in_=row_sum[b][:])
+            v_codes = keep.tile([P, C], U32, name="v_codes%d" % b, align_bytes=64)
+            v_scales = keep.tile([P, C], U8, name="v_scales%d" % b, align_bytes=64)
+            nc.vector.quantize_mx(out=v_codes[:].bitcast(FP8X4), scales=v_scales[:], in_=v_grouped[b][:])
+            e_codes = keep.tile([P, TQ], U32, name="e_codes%d" % b, align_bytes=64)
+            e_scales = keep.tile([P, TQ], U8, name="e_scales%d" % b, align_bytes=64)
+            nc.vector.quantize_mx(out=e_codes[:].bitcast(FP8X4), scales=e_scales[:], in_=e_grouped[b][:])
             out_acc = psum_acc.tile([P, C], F32, name="out_acc", tag="acc")
-            mx_pass(nc, out_acc[:], whole(e_mx), whole(v_mx[b]))
+            mx_pass(nc, out_acc[:], (e_codes[:], e_scales[:]), (v_codes[:], v_scales[:]))
             out_sb = keep.tile([P, C], F32, name="out_sb%d" % b)
-            nc.scalar.activation(out=out_sb[:], in_=out_acc[:], func=ACT.Copy, scale=inv_sum[b][:])
+            if b == 0:
+                nc.scalar.activation(out=out_sb[:], in_=out_acc[:], func=ACT.Copy, scale=inv_sum[:])
+            else:
+                nc.vector.tensor_scalar_mul(out=out_sb[:], in0=out_acc[:], scalar1=inv_sum[:])
             nc.sync.dma_start(out=out[b], in_=out_sb[:])

@@ -19,9 +19,8 @@ P = 128
 PACK = 4
 FLOPS = 3 * 2 * B * TQ * TK * C
 
-K_ORDER = (("var", 0), ("mu", 0), ("var", 1), ("mu", 1))
-HALF_KEYS = TK // 2
-LAG = 4
+K_ORDER = (("var", 0), ("var", 1), ("mu", 0), ("mu", 1))
+HALF = 256
 
 
 def words_to_partitions(nc, bank, rows, ident_f32):
@@ -50,7 +49,6 @@ def tile_probcrossattention_pb_s_kernel(tc, q, k_mu, k_var, v_sample, out):
         psum_acc = ctx.enter_context(tc.psum_pool(name="psum_acc", bufs=4))
         ctx.enter_context(tc.manual_schedule())
 
-        halves = [(kind, b, h) for (kind, b) in K_ORDER for h in range(2)]
         k_dram = {"var": k_var, "mu": k_mu}
 
         q_raw = keep.tile([P, B * C], BF16, name="q_raw")
@@ -60,17 +58,16 @@ def tile_probcrossattention_pb_s_kernel(tc, q, k_mu, k_var, v_sample, out):
         k_raw = {}
         for kind, b in K_ORDER:
             k_raw[(kind, b)] = keep.tile([P, PACK * C], BF16, name="%s_raw%d" % (kind, b))
-        for kind, b, h in halves:
-            cols = slice(h * 2 * C, (h + 1) * 2 * C)
-            nc.sync.dma_start(
-                out=k_raw[(kind, b)][:, cols],
-                in_=k_dram[kind][b].rearrange("(p j) c -> p (j c)", j=PACK)[:, cols],
-            )
-        v_raw = []
+            for h in range(2):
+                cols = slice(h * 2 * C, (h + 1) * 2 * C)
+                nc.sync.dma_start(
+                    out=k_raw[(kind, b)][:, cols],
+                    in_=k_dram[kind][b].rearrange("(p j) c -> p (j c)", j=PACK)[:, cols],
+                )
+        v_raw = {}
         for b in range(B):
-            raw = keep.tile([P, PACK * C], BF16, name="v_raw%d" % b)
-            nc.sync.dma_start(out=raw[:], in_=v_sample[b].rearrange("(p j) c -> p (j c)", j=PACK))
-            v_raw.append(raw)
+            v_raw[b] = keep.tile([P, PACK * C], BF16, name="v_raw%d" % b)
+            nc.sync.dma_start(out=v_raw[b][:], in_=v_sample[b].rearrange("(p j) c -> p (j c)", j=PACK))
 
         ident_f32 = keep.tile([P, P], F32, name="ident_f32")
         make_identity(nc, ident_f32[:])
@@ -99,26 +96,13 @@ def tile_probcrossattention_pb_s_kernel(tc, q, k_mu, k_var, v_sample, out):
             nc.vector.quantize_mx(out=codes[:].bitcast(FP8X4), scales=scales[:], in_=grouped[:])
             q_mx[kind] = (codes, scales)
 
-        k_grouped = {}
-        k_codes = {}
-        k_scales = {}
-        k_acc = {}
-        penalty = {}
-        neg_scores = {}
-        neg_max = {}
-        v_grouped = {}
-        for step in range(len(halves) + LAG):
-            ripe = halves[step - LAG] if step >= LAG else None
-            takes_root = ripe is not None and ripe[0] == "var" and ripe[2] == 1
-            if step < len(halves):
-                kind, b, h = halves[step]
-                x = (kind, b)
-                if h == 0:
-                    k_grouped[x] = keep.tile(
-                        [P, TK * PACK], BF16, name="%s_grouped%d" % x, align_bytes=64
-                    )
-                    k_codes[x] = keep.tile([P, TK], U32, name="%s_codes%d" % x, align_bytes=64)
-                    k_scales[x] = keep.tile([P, TK], U8, name="%s_scales%d" % x, align_bytes=64)
+        k_mx = {}
+        for x in K_ORDER:
+            grouped = keep.tile([P, TK * PACK], BF16, name="%s_grouped%d" % x, align_bytes=64)
+            codes = keep.tile([P, TK], U32, name="%s_codes%d" % x, align_bytes=64)
+            scales = keep.tile([P, TK], U8, name="%s_scales%d" % x, align_bytes=64)
+            k_mx[x] = (codes, scales)
+            for h in range(2):
                 bank = psum_tr.tile([P, 2, 2, P], F32, name="bank", tag="bank")
                 words_to_partitions(
                     nc,
@@ -126,52 +110,55 @@ def tile_probcrossattention_pb_s_kernel(tc, q, k_mu, k_var, v_sample, out):
                     k_raw[x][:].bitcast(F32).rearrange("p (h j u w) -> p h j u w", h=2, j=2, u=2)[:, h],
                     ident_f32,
                 )
-                empty = nc.vector.tensor_copy if takes_root else nc.scalar.copy
-                empty(
-                    out=k_grouped[x][:].bitcast(F32).rearrange("p (h j r u) -> p h j r u", h=2, j=2, u=2)[:, h],
+                nc.scalar.copy(
+                    out=grouped[:].bitcast(F32).rearrange("p (h j r u) -> p h j r u", h=2, j=2, u=2)[:, h],
                     in_=bank[:].rearrange("p j u r -> p j r u"),
                 )
-                keys = slice(h * HALF_KEYS, (h + 1) * HALF_KEYS)
                 nc.vector.quantize_mx(
-                    out=k_codes[x][:, keys].bitcast(FP8X4),
-                    scales=k_scales[x][:, keys],
-                    in_=k_grouped[x][:, h * HALF_KEYS * PACK : (h + 1) * HALF_KEYS * PACK],
+                    out=codes[:, h * HALF : (h + 1) * HALF].bitcast(FP8X4),
+                    scales=scales[:, h * HALF : (h + 1) * HALF],
+                    in_=grouped[:, h * HALF * PACK : (h + 1) * HALF * PACK],
                 )
-            if ripe is not None:
-                kind, b, h = ripe
-                x = (kind, b)
-                if h == 0:
-                    k_acc[x] = psum_acc.tile([P, TK], F32, name="k_acc", tag="acc")
-                keys = slice(h * HALF_KEYS, (h + 1) * HALF_KEYS)
-                queries = slice(b * TQ, (b + 1) * TQ)
-                mx_pass(
-                    nc,
-                    k_acc[x][:, keys],
-                    (q_mx[kind][0][:, queries], q_mx[kind][1][:, queries]),
-                    (k_codes[x][:, keys], k_scales[x][:, keys]),
+
+        v_grouped = {}
+
+        def regroup_values(b):
+            v_grouped[b] = keep.tile([P, C * PACK], BF16, name="v_grouped%d" % b, align_bytes=64)
+            nc.vector.tensor_copy(
+                out=v_grouped[b][:].rearrange("p (c i t) -> p c t i", i=4, t=PACK),
+                in_=v_raw[b][:].rearrange("p (t c i) -> p c t i", t=PACK, i=4),
+            )
+
+        regroup_values(0)
+
+        penalty = {}
+        neg_scores = {}
+        neg_max = {}
+        for kind, b in K_ORDER:
+            acc = psum_acc.tile([P, TK], F32, name="k_acc", tag="acc")
+            queries = slice(b * TQ, (b + 1) * TQ)
+            mx_pass(
+                nc,
+                acc[:],
+                (q_mx[kind][0][:, queries], q_mx[kind][1][:, queries]),
+                (k_mx[(kind, b)][0][:], k_mx[(kind, b)][1][:]),
+            )
+            if kind == "var":
+                penalty[b] = keep.tile([P, TK], F32, name="penalty%d" % b)
+                nc.scalar.activation(out=penalty[b][:], in_=acc[:], func=ACT.Sqrt, scale=BETA * BETA / C)
+            else:
+                neg_scores[b] = keep.tile([P, TK], F32, name="neg_scores%d" % b)
+                nc.vector.scalar_tensor_tensor(
+                    out=neg_scores[b][:],
+                    in0=acc[:],
+                    scalar=-1.0 / math.sqrt(C),
+                    in1=penalty[b][:],
+                    op0=ALU.mult,
+                    op1=ALU.add,
                 )
-                if h == 1 and kind == "var":
-                    penalty[b] = keep.tile([P, TK], F32, name="penalty%d" % b)
-                    nc.scalar.activation(
-                        out=penalty[b][:], in_=k_acc[x][:], func=ACT.Sqrt, scale=BETA * BETA / C
-                    )
-                if h == 1 and kind == "mu":
-                    neg_scores[b] = keep.tile([P, TK], F32, name="neg_scores%d" % b)
-                    nc.vector.scalar_tensor_tensor(
-                        out=neg_scores[b][:],
-                        in0=k_acc[x][:],
-                        scalar=-1.0 / math.sqrt(C),
-                        in1=penalty[b][:],
-                        op0=ALU.mult,
-                        op1=ALU.add,
-                    )
-                    neg_max[b] = keep.tile([P, 1], F32, name="neg_max%d" % b)
-                    nc.vector.tensor_reduce(out=neg_max[b][:], in_=neg_scores[b][:], axis=AX.X, op=ALU.min)
-                    v_grouped[b] = keep.tile([P, C * PACK], BF16, name="v_grouped%d" % b, align_bytes=64)
-                    nc.vector.tensor_copy(
-                        out=v_grouped[b][:].rearrange("p (c i t) -> p c t i", i=4, t=PACK),
-                        in_=v_raw[b][:].rearrange("p (t c i) -> p c t i", t=PACK, i=4),
-                    )
+                neg_max[b] = keep.tile([P, 1], F32, name="neg_max%d" % b)
+                nc.vector.tensor_reduce(out=neg_max[b][:], in_=neg_scores[b][:], axis=AX.X, op=ALU.min)
+        regroup_values(1)
 
         warm_exp = keep.tile([P, 1], F32, name="warm_exp")
         nc.scalar.activation(out=warm_exp[:], in_=one[:], func=ACT.Exp)
@@ -199,20 +186,31 @@ def tile_probcrossattention_pb_s_kernel(tc, q, k_mu, k_var, v_sample, out):
                 in_=e_t[b][:].rearrange("p t r -> p r t"),
             )
 
+        out_acc = {}
         for b in range(B):
-            inv_sum = keep.tile([P, 1], F32, name="inv_sum%d" % b)
-            nc.vector.reciprocal(out=inv_sum[:], in_=row_sum[b][:])
             v_codes = keep.tile([P, C], U32, name="v_codes%d" % b, align_bytes=64)
             v_scales = keep.tile([P, C], U8, name="v_scales%d" % b, align_bytes=64)
             nc.vector.quantize_mx(out=v_codes[:].bitcast(FP8X4), scales=v_scales[:], in_=v_grouped[b][:])
             e_codes = keep.tile([P, TQ], U32, name="e_codes%d" % b, align_bytes=64)
             e_scales = keep.tile([P, TQ], U8, name="e_scales%d" % b, align_bytes=64)
             nc.vector.quantize_mx(out=e_codes[:].bitcast(FP8X4), scales=e_scales[:], in_=e_grouped[b][:])
-            out_acc = psum_acc.tile([P, C], F32, name="out_acc", tag="acc")
-            mx_pass(nc, out_acc[:], (e_codes[:], e_scales[:]), (v_codes[:], v_scales[:]))
-            out_sb = keep.tile([P, C], F32, name="out_sb%d" % b)
-            if b == 0:
-                nc.scalar.activation(out=out_sb[:], in_=out_acc[:], func=ACT.Copy, scale=inv_sum[:])
-            else:
-                nc.vector.tensor_scalar_mul(out=out_sb[:], in0=out_acc[:], scalar1=inv_sum[:])
-            nc.sync.dma_start(out=out[b], in_=out_sb[:])
+            for h in range(2):
+                channels = slice(h * HALF, (h + 1) * HALF)
+                out_acc[(b, h)] = psum_acc.tile([P, HALF], F32, name="out_acc", tag="acc")
+                mx_pass(
+                    nc,
+                    out_acc[(b, h)][:],
+                    (e_codes[:], e_scales[:]),
+                    (v_codes[:, channels], v_scales[:, channels]),
+                )
+        inv_sum = {}
+        for b in range(B):
+            inv_sum[b] = keep.tile([P, 1], F32, name="inv_sum%d" % b)
+            nc.vector.reciprocal(out=inv_sum[b][:], in_=row_sum[b][:])
+        for b in range(B):
+            first = keep.tile([P, HALF], F32, name="out_first%d" % b)
+            nc.scalar.activation(out=first[:], in_=out_acc[(b, 0)][:], func=ACT.Copy, scale=inv_sum[b][:])
+            nc.sync.dma_start(out=out[b][:, 0:HALF], in_=first[:])
+            second = keep.tile([P, HALF], F32, name="out_second%d" % b)
+            nc.vector.tensor_scalar_mul(out=second[:], in0=out_acc[(b, 1)][:], scalar1=inv_sum[b][:])
+            nc.sync.dma_start(out=out[b][:, HALF:C], in_=second[:])

@@ -156,8 +156,9 @@ def tile_probcrossattention_pb_s_kernel(tc, q, k_mu, k_var, v_sample, out):
                     op0=ALU.mult,
                     op1=ALU.add,
                 )
-                neg_max[b] = keep.tile([P, 1], F32, name="neg_max%d" % b)
-                nc.vector.tensor_reduce(out=neg_max[b][:], in_=neg_scores[b][:], axis=AX.X, op=ALU.min)
+        for b in range(B):
+            neg_max[b] = keep.tile([P, 1], F32, name="neg_max%d" % b)
+            nc.vector.tensor_reduce(out=neg_max[b][:], in_=neg_scores[b][:], axis=AX.X, op=ALU.min)
         regroup_values(1)
 
         warm_exp = keep.tile([P, 1], F32, name="warm_exp")

@@ -121,15 +121,26 @@ def tile_probcrossattention_pb_s_kernel(tc, q, k_mu, k_var, v_sample, out):
                 )
 
         v_grouped = {}
-
-        def regroup_values(b):
+        for b in range(B):
             v_grouped[b] = keep.tile([P, C * PACK], BF16, name="v_grouped%d" % b, align_bytes=64)
+
+        def regroup_values(b, c0, c1):
             nc.vector.tensor_copy(
-                out=v_grouped[b][:].rearrange("p (c i t) -> p c t i", i=4, t=PACK),
-                in_=v_raw[b][:].rearrange("p (t c i) -> p c t i", t=PACK, i=4),
+                out=v_grouped[b][:, c0 * PACK : c1 * PACK].rearrange("p (c i t) -> p c t i", i=4, t=PACK),
+                in_=v_raw[b][:].rearrange("p (t c i) -> p c t i", t=PACK, i=4)[:, c0 // 4 : c1 // 4],
             )
 
-        regroup_values(0)
+        gate = keep.tile([P, 1], F32, name="gate")
+        nc.vector.memset(gate[:], 1.0)
+        for i in range(3):
+            nc.gpsimd.tensor_scalar(
+                out=v_grouped[0][:, i * P * PACK : (i + 1) * P * PACK].rearrange("p (c t) -> p c t", t=PACK),
+                in0=v_raw[0][:].rearrange("p (t c) -> p c t", t=PACK)[:, i * P : (i + 1) * P],
+                scalar1=gate[:],
+                scalar2=0.0,
+                op0=ALU.mult,
+                op1=ALU.add,
+            )
 
         penalty = {}
         neg_scores = {}
@@ -159,7 +170,8 @@ def tile_probcrossattention_pb_s_kernel(tc, q, k_mu, k_var, v_sample, out):
         for b in range(B):
             neg_max[b] = keep.tile([P, 1], F32, name="neg_max%d" % b)
             nc.vector.tensor_reduce(out=neg_max[b][:], in_=neg_scores[b][:], axis=AX.X, op=ALU.min)
-        regroup_values(1)
+        regroup_values(0, 3 * P, C)
+        regroup_values(1, 0, C)
 
         warm_exp = keep.tile([P, 1], F32, name="warm_exp")
         nc.scalar.activation(out=warm_exp[:], in_=one[:], func=ACT.Exp)

@@ -21,12 +21,7 @@ FLOPS = 3 * 2 * B * TQ * TK * C
 
 K_ORDER = (("var", 0), ("var", 1), ("mu", 0), ("mu", 1))
 HALF = 256
-
-
-def words_to_partitions(nc, bank, rows, ident_f32):
-    for g in range(2):
-        for u in range(2):
-            nc.tensor.transpose(bank[:, g, u, :], rows[:, g, u, :], ident_f32[:])
+QUARTER = 128
 
 
 def mx_pass(nc, acc, stationary, moving):
@@ -49,181 +44,270 @@ def tile_probcrossattention_pb_s_kernel(tc, q, k_mu, k_var, v_sample, out):
         psum_acc = ctx.enter_context(tc.psum_pool(name="psum_acc", bufs=4))
         ctx.enter_context(tc.manual_schedule())
 
-        k_dram = {"var": k_var, "mu": k_mu}
+        def sbuf(shape, dtype, name):
+            return keep.tile(shape, dtype, name=name, align_bytes=64)
 
-        q_raw = keep.tile([P, B * C], BF16, name="q_raw")
+        q_raw = sbuf([P, B * C], BF16, "q_raw")
         nc.sync.dma_start(
             out=q_raw[:].rearrange("p (b c) -> p b c", b=B), in_=q.rearrange("b q c -> q b c")
         )
+        k_dram = {"var": k_var, "mu": k_mu}
         k_raw = {}
-        for kind, b in K_ORDER:
-            k_raw[(kind, b)] = keep.tile([P, PACK * C], BF16, name="%s_raw%d" % (kind, b))
+        for x in K_ORDER:
+            k_raw[x] = sbuf([P, PACK * C], BF16, "%s_raw%d" % x)
             for h in range(2):
                 cols = slice(h * 2 * C, (h + 1) * 2 * C)
                 nc.sync.dma_start(
-                    out=k_raw[(kind, b)][:, cols],
-                    in_=k_dram[kind][b].rearrange("(p j) c -> p (j c)", j=PACK)[:, cols],
+                    out=k_raw[x][:, cols],
+                    in_=k_dram[x[0]][x[1]].rearrange("(p j) c -> p (j c)", j=PACK)[:, cols],
                 )
         v_raw = {}
         for b in range(B):
-            v_raw[b] = keep.tile([P, PACK * C], BF16, name="v_raw%d" % b)
+            v_raw[b] = sbuf([P, PACK * C], BF16, "v_raw%d" % b)
             nc.sync.dma_start(out=v_raw[b][:], in_=v_sample[b].rearrange("(p j) c -> p (j c)", j=PACK))
 
-        ident_f32 = keep.tile([P, P], F32, name="ident_f32")
+        ident_f32 = sbuf([P, P], F32, "ident_f32")
         make_identity(nc, ident_f32[:])
-        ident_bf16 = keep.tile([P, P], BF16, name="ident_bf16")
+        ident_bf16 = sbuf([P, P], BF16, "ident_bf16")
         make_identity(nc, ident_bf16[:])
-        one = keep.tile([P, 1], F32, name="one")
+        one = sbuf([P, 1], F32, "one")
         nc.vector.memset(one[:], 1.0)
-        warm_sqrt = keep.tile([P, 1], F32, name="warm_sqrt")
+        warm_sqrt = sbuf([P, 1], F32, "warm_sqrt")
         nc.scalar.activation(out=warm_sqrt[:], in_=one[:], func=ACT.Sqrt)
 
-        q_bank = psum_tr.tile([P, B, 2, P], F32, name="q_bank", tag="bank")
-        words_to_partitions(
-            nc, q_bank, q_raw[:].bitcast(F32).rearrange("p (b u w) -> p b u w", b=B, u=2), ident_f32
-        )
-        q_grouped = keep.tile([P, B * TQ * PACK], BF16, name="q_grouped", align_bytes=64)
-        nc.scalar.copy(
-            out=q_grouped[:].bitcast(F32).rearrange("p (b r u) -> p b r u", b=B, u=2),
-            in_=q_bank[:].rearrange("p b u r -> p b r u"),
-        )
-        q2_grouped = keep.tile([P, B * TQ * PACK], BF16, name="q2_grouped", align_bytes=64)
-        nc.vector.tensor_tensor(out=q2_grouped[:], in0=q_grouped[:], in1=q_grouped[:], op=ALU.mult)
-        q_mx = {}
-        for kind, grouped in (("mu", q_grouped), ("var", q2_grouped)):
-            codes = keep.tile([P, B * TQ], U32, name="q_codes_" + kind, align_bytes=64)
-            scales = keep.tile([P, B * TQ], U8, name="q_scales_" + kind, align_bytes=64)
-            nc.vector.quantize_mx(out=codes[:].bitcast(FP8X4), scales=scales[:], in_=grouped[:])
-            q_mx[kind] = (codes, scales)
-
-        k_mx = {}
+        q_grouped = sbuf([P, B * TQ * PACK], BF16, "q_grouped")
+        q2_grouped = sbuf([P, B * TQ * PACK], BF16, "q2_grouped")
+        q_grouped_of = {"mu": q_grouped, "var": q2_grouped}
+        q_codes = {}
+        q_scales = {}
+        for kind in ("mu", "var"):
+            q_codes[kind] = sbuf([P, B * TQ], U32, "q_codes_" + kind)
+            q_scales[kind] = sbuf([P, B * TQ], U8, "q_scales_" + kind)
+        k_grouped = {}
+        k_codes = {}
+        k_scales = {}
         for x in K_ORDER:
-            grouped = keep.tile([P, TK * PACK], BF16, name="%s_grouped%d" % x, align_bytes=64)
-            codes = keep.tile([P, TK], U32, name="%s_codes%d" % x, align_bytes=64)
-            scales = keep.tile([P, TK], U8, name="%s_scales%d" % x, align_bytes=64)
-            k_mx[x] = (codes, scales)
-            for h in range(2):
-                bank = psum_tr.tile([P, 2, 2, P], F32, name="bank", tag="bank")
-                words_to_partitions(
-                    nc,
-                    bank,
-                    k_raw[x][:].bitcast(F32).rearrange("p (h j u w) -> p h j u w", h=2, j=2, u=2)[:, h],
-                    ident_f32,
-                )
-                nc.scalar.copy(
-                    out=grouped[:].bitcast(F32).rearrange("p (h j r u) -> p h j r u", h=2, j=2, u=2)[:, h],
-                    in_=bank[:].rearrange("p j u r -> p j r u"),
-                )
-                nc.vector.quantize_mx(
-                    out=codes[:, h * HALF : (h + 1) * HALF].bitcast(FP8X4),
-                    scales=scales[:, h * HALF : (h + 1) * HALF],
-                    in_=grouped[:, h * HALF * PACK : (h + 1) * HALF * PACK],
-                )
-
+            k_grouped[x] = sbuf([P, TK * PACK], BF16, "%s_grouped%d" % x)
+            k_codes[x] = sbuf([P, TK], U32, "%s_codes%d" % x)
+            k_scales[x] = sbuf([P, TK], U8, "%s_scales%d" % x)
         v_grouped = {}
+        v_codes = {}
+        v_scales = {}
+        e_bf16 = {}
+        e_grouped = {}
+        e_codes = {}
+        e_scales = {}
+        penalty = {}
+        neg_scores = {}
+        neg_max = {}
+        row_sum = {}
+        inv_sum = {}
         for b in range(B):
-            v_grouped[b] = keep.tile([P, C * PACK], BF16, name="v_grouped%d" % b, align_bytes=64)
+            v_grouped[b] = sbuf([P, C * PACK], BF16, "v_grouped%d" % b)
+            v_codes[b] = sbuf([P, C], U32, "v_codes%d" % b)
+            v_scales[b] = sbuf([P, C], U8, "v_scales%d" % b)
+            e_bf16[b] = sbuf([P, TK], BF16, "e_bf16_%d" % b)
+            e_grouped[b] = sbuf([P, TQ * PACK], BF16, "e_grouped%d" % b)
+            e_codes[b] = sbuf([P, TQ], U32, "e_codes%d" % b)
+            e_scales[b] = sbuf([P, TQ], U8, "e_scales%d" % b)
+            penalty[b] = sbuf([P, TK], F32, "penalty%d" % b)
+            neg_scores[b] = sbuf([P, TK], F32, "neg_scores%d" % b)
+            neg_max[b] = sbuf([P, 1], F32, "neg_max%d" % b)
+            row_sum[b] = sbuf([P, 1], F32, "row_sum%d" % b)
+            inv_sum[b] = sbuf([P, 1], F32, "inv_sum%d" % b)
+        banks = {}
+        k_acc = {}
+        out_acc = {}
 
-        def regroup_values(b, c0, c1):
-            nc.vector.tensor_copy(
-                out=v_grouped[b][:, c0 * PACK : c1 * PACK].rearrange("p (c i t) -> p c t i", i=4, t=PACK),
-                in_=v_raw[b][:].rearrange("p (t c i) -> p c t i", t=PACK, i=4)[:, c0 // 4 : c1 // 4],
+        def q_transposes():
+            banks["q"] = psum_tr.tile([P, B, 2, P], F32, name="q_bank", tag="bank")
+            words = q_raw[:].bitcast(F32).rearrange("p (b u w) -> p b u w", b=B, u=2)
+            for b in range(B):
+                for u in range(2):
+                    nc.tensor.transpose(banks["q"][:, b, u, :], words[:, b, u, :], ident_f32[:])
+
+        def q_copy(copy):
+            copy(
+                out=q_grouped[:].bitcast(F32).rearrange("p (b r u) -> p b r u", b=B, u=2),
+                in_=banks["q"][:].rearrange("p b u r -> p b r u"),
             )
 
-        gate = keep.tile([P, 1], F32, name="gate")
-        nc.vector.memset(gate[:], 1.0)
-        for i in range(3):
-            nc.gpsimd.tensor_scalar(
-                out=v_grouped[0][:, i * P * PACK : (i + 1) * P * PACK].rearrange("p (c t) -> p c t", t=PACK),
-                in0=v_raw[0][:].rearrange("p (t c) -> p c t", t=PACK)[:, i * P : (i + 1) * P],
-                scalar1=gate[:],
-                scalar2=0.0,
+        def q_square():
+            nc.vector.tensor_tensor(out=q2_grouped[:], in0=q_grouped[:], in1=q_grouped[:], op=ALU.mult)
+
+        def q_quantise(kind):
+            nc.vector.quantize_mx(
+                out=q_codes[kind][:].bitcast(FP8X4), scales=q_scales[kind][:], in_=q_grouped_of[kind][:]
+            )
+
+        def k_transposes(x, h):
+            banks[x + (h,)] = psum_tr.tile([P, 2, 2, P], F32, name="bank", tag="bank")
+            words = k_raw[x][:].bitcast(F32).rearrange("p (h j u w) -> p h j u w", h=2, j=2, u=2)
+            for j in range(2):
+                for u in range(2):
+                    nc.tensor.transpose(banks[x + (h,)][:, j, u, :], words[:, h, j, u, :], ident_f32[:])
+
+        def k_copy(copy, x, h):
+            copy(
+                out=k_grouped[x][:].bitcast(F32).rearrange("p (h j r u) -> p h j r u", h=2, j=2, u=2)[:, h],
+                in_=banks[x + (h,)][:].rearrange("p j u r -> p j r u"),
+            )
+
+        def k_quantise(x, h):
+            keys = slice(h * HALF, (h + 1) * HALF)
+            nc.vector.quantize_mx(
+                out=k_codes[x][:, keys].bitcast(FP8X4),
+                scales=k_scales[x][:, keys],
+                in_=k_grouped[x][:, h * HALF * PACK : (h + 1) * HALF * PACK],
+            )
+
+        def k_matmul(x):
+            kind, b = x
+            k_acc[x] = psum_acc.tile([P, TK], F32, name="k_acc", tag="acc")
+            queries = slice(b * TQ, (b + 1) * TQ)
+            mx_pass(
+                nc,
+                k_acc[x][:],
+                (q_codes[kind][:, queries], q_scales[kind][:, queries]),
+                (k_codes[x][:], k_scales[x][:]),
+            )
+
+        def penalty_sqrt(b):
+            nc.scalar.activation(
+                out=penalty[b][:], in_=k_acc[("var", b)][:], func=ACT.Sqrt, scale=BETA * BETA / C
+            )
+
+        def scores(b):
+            nc.vector.scalar_tensor_tensor(
+                out=neg_scores[b][:],
+                in0=k_acc[("mu", b)][:],
+                scalar=-1.0 / math.sqrt(C),
+                in1=penalty[b][:],
                 op0=ALU.mult,
                 op1=ALU.add,
             )
 
-        penalty = {}
-        neg_scores = {}
-        neg_max = {}
-        for kind, b in K_ORDER:
-            acc = psum_acc.tile([P, TK], F32, name="k_acc", tag="acc")
-            queries = slice(b * TQ, (b + 1) * TQ)
-            mx_pass(
-                nc,
-                acc[:],
-                (q_mx[kind][0][:, queries], q_mx[kind][1][:, queries]),
-                (k_mx[(kind, b)][0][:], k_mx[(kind, b)][1][:]),
-            )
-            if kind == "var":
-                penalty[b] = keep.tile([P, TK], F32, name="penalty%d" % b)
-                nc.scalar.activation(out=penalty[b][:], in_=acc[:], func=ACT.Sqrt, scale=BETA * BETA / C)
-            else:
-                neg_scores[b] = keep.tile([P, TK], F32, name="neg_scores%d" % b)
-                nc.vector.scalar_tensor_tensor(
-                    out=neg_scores[b][:],
-                    in0=acc[:],
-                    scalar=-1.0 / math.sqrt(C),
-                    in1=penalty[b][:],
-                    op0=ALU.mult,
-                    op1=ALU.add,
-                )
-        for b in range(B):
-            neg_max[b] = keep.tile([P, 1], F32, name="neg_max%d" % b)
+        def scores_min(b):
             nc.vector.tensor_reduce(out=neg_max[b][:], in_=neg_scores[b][:], axis=AX.X, op=ALU.min)
-        regroup_values(0, 3 * P, C)
-        regroup_values(1, 0, C)
 
-        warm_exp = keep.tile([P, 1], F32, name="warm_exp")
-        nc.scalar.activation(out=warm_exp[:], in_=one[:], func=ACT.Exp)
-        row_sum = {}
-        e_t = {}
-        for b in range(B):
-            e_bf16 = keep.tile([P, TK], BF16, name="e_bf16_%d" % b)
-            row_sum[b] = keep.tile([P, 1], F32, name="row_sum%d" % b)
+        def v_regroup(copy, b, c0, c1):
+            copy(
+                out=v_grouped[b][:, c0 * PACK : c1 * PACK].rearrange("p (c i t) -> p c t i", i=4, t=PACK),
+                in_=v_raw[b][:].rearrange("p (t c i) -> p c t i", t=PACK, i=4)[:, c0 // 4 : c1 // 4],
+            )
+
+        def v_quantise(b):
+            nc.vector.quantize_mx(
+                out=v_codes[b][:].bitcast(FP8X4), scales=v_scales[b][:], in_=v_grouped[b][:]
+            )
+
+        def e_exp(b):
             nc.scalar.activation(
-                out=e_bf16[:],
+                out=e_bf16[b][:],
                 in_=neg_scores[b][:],
                 func=ACT.Exp,
                 bias=neg_max[b][:],
                 scale=-1.0,
                 accum_out=row_sum[b][:],
             )
-            e_t[b] = psum_tr.tile([P, PACK, TQ], BF16, name="e_t", tag="bank")
+
+        def e_transposes(b):
+            banks[("e", b)] = psum_tr.tile([P, PACK, TQ], BF16, name="e_t", tag="bank")
             for t in range(PACK):
-                nc.tensor.transpose(e_t[b][:, t, :], e_bf16[:, t * P : (t + 1) * P], ident_bf16[:])
-        e_grouped = {}
-        for b in range(B):
-            e_grouped[b] = keep.tile([P, TQ * PACK], BF16, name="e_grouped%d" % b, align_bytes=64)
+                nc.tensor.transpose(
+                    banks[("e", b)][:, t, :], e_bf16[b][:, t * P : (t + 1) * P], ident_bf16[:]
+                )
+
+        def e_copy(b):
             nc.scalar.copy(
                 out=e_grouped[b][:].rearrange("p (r t) -> p r t", t=PACK),
-                in_=e_t[b][:].rearrange("p t r -> p r t"),
+                in_=banks[("e", b)][:].rearrange("p t r -> p r t"),
             )
 
-        out_acc = {}
-        for b in range(B):
-            v_codes = keep.tile([P, C], U32, name="v_codes%d" % b, align_bytes=64)
-            v_scales = keep.tile([P, C], U8, name="v_scales%d" % b, align_bytes=64)
-            nc.vector.quantize_mx(out=v_codes[:].bitcast(FP8X4), scales=v_scales[:], in_=v_grouped[b][:])
-            e_codes = keep.tile([P, TQ], U32, name="e_codes%d" % b, align_bytes=64)
-            e_scales = keep.tile([P, TQ], U8, name="e_scales%d" % b, align_bytes=64)
-            nc.vector.quantize_mx(out=e_codes[:].bitcast(FP8X4), scales=e_scales[:], in_=e_grouped[b][:])
+        def e_quantise(b):
+            nc.vector.quantize_mx(
+                out=e_codes[b][:].bitcast(FP8X4), scales=e_scales[b][:], in_=e_grouped[b][:]
+            )
+
+        def out_matmul(b, h):
+            channels = slice(h * HALF, (h + 1) * HALF)
+            out_acc[(b, h)] = psum_acc.tile([P, HALF], F32, name="out_acc", tag="acc")
+            mx_pass(
+                nc,
+                out_acc[(b, h)][:],
+                (e_codes[b][:], e_scales[b][:]),
+                (v_codes[b][:, channels], v_scales[b][:, channels]),
+            )
+
+        def out_store(on_vector, b, h):
+            channels = slice(h * HALF, (h + 1) * HALF)
+            result = sbuf([P, HALF], F32, "out%d_%d" % (b, h))
+            if on_vector:
+                nc.vector.tensor_scalar_mul(out=result[:], in0=out_acc[(b, h)][:], scalar1=inv_sum[b][:])
+            else:
+                nc.scalar.activation(out=result[:], in_=out_acc[(b, h)][:], func=ACT.Copy, scale=inv_sum[b][:])
+            nc.sync.dma_start(out=out[b][:, channels], in_=result[:])
+
+        on_scalar = nc.scalar.copy
+        on_vector = nc.vector.tensor_copy
+        var0, var1, mu0, mu1 = K_ORDER
+
+        q_transposes()
+        q_copy(on_scalar)
+        q_square()
+        q_quantise("mu")
+        q_quantise("var")
+
+        for x in (var0, var1, mu0):
             for h in range(2):
-                channels = slice(h * HALF, (h + 1) * HALF)
-                out_acc[(b, h)] = psum_acc.tile([P, HALF], F32, name="out_acc", tag="acc")
-                mx_pass(
-                    nc,
-                    out_acc[(b, h)][:],
-                    (e_codes[:], e_scales[:]),
-                    (v_codes[:, channels], v_scales[:, channels]),
-                )
-        inv_sum = {}
+                k_transposes(x, h)
+                k_copy(on_scalar, x, h)
+                k_quantise(x, h)
+        for h in range(2):
+            k_transposes(mu1, h)
+        k_copy(on_scalar, mu1, 0)
+        k_copy(on_vector, mu1, 1)
+        for h in range(2):
+            k_quantise(mu1, h)
+        for x in K_ORDER:
+            k_matmul(x)
         for b in range(B):
-            inv_sum[b] = keep.tile([P, 1], F32, name="inv_sum%d" % b)
+            penalty_sqrt(b)
+        warm_exp = sbuf([P, 1], F32, "warm_exp")
+        nc.scalar.activation(out=warm_exp[:], in_=one[:], func=ACT.Exp)
+
+        gate = sbuf([P, 1], F32, "gate")
+        nc.vector.memset(gate[:], 1.0)
+        for i in range(3):
+            nc.gpsimd.tensor_scalar(
+                out=v_grouped[0][:, i * QUARTER * PACK : (i + 1) * QUARTER * PACK].rearrange(
+                    "p (c t) -> p c t", t=PACK
+                ),
+                in0=v_raw[0][:].rearrange("p (t c) -> p c t", t=PACK)[:, i * QUARTER : (i + 1) * QUARTER],
+                scalar1=gate[:],
+                scalar2=0.0,
+                op0=ALU.mult,
+                op1=ALU.add,
+            )
+        for b in range(B):
+            scores(b)
+        for b in range(B):
+            scores_min(b)
+            e_exp(b)
+            e_transposes(b)
+        v_regroup(on_scalar, 1, 3 * QUARTER, C)
+        for b in range(B):
+            e_copy(b)
+        v_regroup(on_vector, 0, 3 * QUARTER, C)
+        v_regroup(on_vector, 1, 0, 3 * QUARTER)
+        for b in range(B):
+            v_quantise(b)
+        for b in range(B):
             nc.vector.reciprocal(out=inv_sum[b][:], in_=row_sum[b][:])
         for b in range(B):
-            first = keep.tile([P, HALF], F32, name="out_first%d" % b)
-            nc.scalar.activation(out=first[:], in_=out_acc[(b, 0)][:], func=ACT.Copy, scale=inv_sum[b][:])
-            nc.sync.dma_start(out=out[b][:, 0:HALF], in_=first[:])
-            second = keep.tile([P, HALF], F32, name="out_second%d" % b)
-            nc.vector.tensor_scalar_mul(out=second[:], in0=out_acc[(b, 1)][:], scalar1=inv_sum[b][:])
-            nc.sync.dma_start(out=out[b][:, HALF:C], in_=second[:])
+            e_quantise(b)
+            for h in range(2):
+                out_matmul(b, h)
+        for b in range(B):
+            for h in range(2):
+                out_store(h == 1, b, h)

@@ -66,6 +66,17 @@ def tile_probcrossattention_pb_s_kernel(tc, q, k_mu, k_var, v_sample, out):
             v_raw[b] = sbuf([P, PACK * C], BF16, "v_raw%d" % b)
             nc.sync.dma_start(out=v_raw[b][:], in_=v_sample[b].rearrange("(p j) c -> p (j c)", j=PACK))
 
+        zeros = sbuf([P, TK], BF16, "zeros")
+        nc.vector.memset(zeros[:], 0.0)
+        zero_codes = sbuf([P, TK // PACK], U32, "zero_codes")
+        zero_scales = sbuf([P, TK // PACK], U8, "zero_scales")
+        nc.vector.quantize_mx(out=zero_codes[:].bitcast(FP8X4), scales=zero_scales[:], in_=zeros[:])
+        warm = psum_acc.tile([P, TK], F32, name="warm", tag="acc")
+        for i in range(2):
+            nc.tensor.matmul(warm[:], lhsT=zeros[:, 0:P], rhs=zeros[:], start=True, stop=True)
+        for i in range(6):
+            mx_pass(nc, warm[:, 0:P], (zero_codes[:], zero_scales[:]), (zero_codes[:], zero_scales[:]))
+
         ident_f32 = sbuf([P, P], F32, "ident_f32")
         make_identity(nc, ident_f32[:])
         ident_bf16 = sbuf([P, P], BF16, "ident_bf16")
@@ -248,6 +259,16 @@ def tile_probcrossattention_pb_s_kernel(tc, q, k_mu, k_var, v_sample, out):
                 nc.scalar.activation(out=result[:], in_=out_acc[(b, h)][:], func=ACT.Copy, scale=inv_sum[b][:])
             nc.sync.dma_start(out=out[b][:, channels], in_=result[:])
 
+        def busy_passes(n):
+            again = psum_acc.tile([P, TK], F32, name="again", tag="acc")
+            for i in range(n):
+                mx_pass(
+                    nc,
+                    again[:],
+                    (q_codes["var"][:, 0:TQ], q_scales["var"][:, 0:TQ]),
+                    (k_codes[("var", 0)][:], k_scales[("var", 0)][:]),
+                )
+
         on_scalar = nc.scalar.copy
         on_vector = nc.vector.tensor_copy
         var0, var1, mu0, mu1 = K_ORDER
@@ -291,10 +312,13 @@ def tile_probcrossattention_pb_s_kernel(tc, q, k_mu, k_var, v_sample, out):
             )
         for b in range(B):
             scores(b)
+        for n in (1, 1, 1, 2):
+            busy_passes(n)
         for b in range(B):
             scores_min(b)
             e_exp(b)
             e_transposes(b)
+        busy_passes(2)
         v_regroup(on_scalar, 1, 3 * QUARTER, C)
         for b in range(B):
             e_copy(b)

@@ -79,8 +79,6 @@ def tile_probcrossattention_pb_s_kernel(tc, q, k_mu, k_var, v_sample, out):
 
         ident_f32 = sbuf([P, P], F32, "ident_f32")
         make_identity(nc, ident_f32[:])
-        ident_bf16 = sbuf([P, P], BF16, "ident_bf16")
-        make_identity(nc, ident_bf16[:])
         one = sbuf([P, 1], F32, "one")
         nc.vector.memset(one[:], 1.0)
         warm_sqrt = sbuf([P, 1], F32, "warm_sqrt")
@@ -111,8 +109,8 @@ def tile_probcrossattention_pb_s_kernel(tc, q, k_mu, k_var, v_sample, out):
         penalty = {}
         neg_scores = {}
         neg_max = {}
-        row_sum = {}
-        inv_sum = {}
+        row_sum = sbuf([P, B], F32, "row_sum")
+        inv_sum = sbuf([P, B], F32, "inv_sum")
         for b in range(B):
             v_grouped[b] = sbuf([P, C * PACK], BF16, "v_grouped%d" % b)
             v_codes[b] = sbuf([P, C], U32, "v_codes%d" % b)
@@ -124,8 +122,6 @@ def tile_probcrossattention_pb_s_kernel(tc, q, k_mu, k_var, v_sample, out):
             penalty[b] = sbuf([P, TK], F32, "penalty%d" % b)
             neg_scores[b] = sbuf([P, TK], F32, "neg_scores%d" % b)
             neg_max[b] = sbuf([P, 1], F32, "neg_max%d" % b)
-            row_sum[b] = sbuf([P, 1], F32, "row_sum%d" % b)
-            inv_sum[b] = sbuf([P, 1], F32, "inv_sum%d" % b)
         banks = {}
         k_acc = {}
         out_acc = {}
@@ -160,8 +156,8 @@ def tile_probcrossattention_pb_s_kernel(tc, q, k_mu, k_var, v_sample, out):
 
         def k_copy(copy, x, h):
             copy(
-                out=k_grouped[x][:].bitcast(F32).rearrange("p (h j r u) -> p h j r u", h=2, j=2, u=2)[:, h],
-                in_=banks[x + (h,)][:].rearrange("p j u r -> p j r u"),
+                out=k_grouped[x][:].bitcast(F32).rearrange("p (h r j u) -> p h r j u", h=2, j=2, u=2)[:, h],
+                in_=banks[x + (h,)][:].rearrange("p j u r -> p r j u"),
             )
 
         def k_quantise(x, h):
@@ -219,20 +215,22 @@ def tile_probcrossattention_pb_s_kernel(tc, q, k_mu, k_var, v_sample, out):
                 func=ACT.Exp,
                 bias=neg_max[b][:],
                 scale=-1.0,
-                accum_out=row_sum[b][:],
+                accum_out=row_sum[:, b : b + 1],
             )
 
         def e_transposes(b):
-            banks[("e", b)] = psum_tr.tile([P, PACK, TQ], BF16, name="e_t", tag="bank")
-            for t in range(PACK):
+            banks[("e", b)] = psum_tr.tile([P, 2, TQ], F32, name="e_t", tag="bank")
+            for u in range(2):
                 nc.tensor.transpose(
-                    banks[("e", b)][:, t, :], e_bf16[b][:, t * P : (t + 1) * P], ident_bf16[:]
+                    banks[("e", b)][:, u, :],
+                    e_bf16[b][:].bitcast(F32)[:, u * P : (u + 1) * P],
+                    ident_f32[:],
                 )
 
         def e_copy(b):
             nc.scalar.copy(
-                out=e_grouped[b][:].rearrange("p (r t) -> p r t", t=PACK),
-                in_=banks[("e", b)][:].rearrange("p t r -> p r t"),
+                out=e_grouped[b][:].bitcast(F32).rearrange("p (r u) -> p r u", u=2),
+                in_=banks[("e", b)][:].rearrange("p u r -> p r u"),
             )
 
         def e_quantise(b):
@@ -254,9 +252,9 @@ def tile_probcrossattention_pb_s_kernel(tc, q, k_mu, k_var, v_sample, out):
             channels = slice(h * HALF, (h + 1) * HALF)
             result = sbuf([P, HALF], F32, "out%d_%d" % (b, h))
             if on_vector:
-                nc.vector.tensor_scalar_mul(out=result[:], in0=out_acc[(b, h)][:], scalar1=inv_sum[b][:])
+                nc.vector.tensor_scalar_mul(out=result[:], in0=out_acc[(b, h)][:], scalar1=inv_sum[:, b : b + 1])
             else:
-                nc.scalar.activation(out=result[:], in_=out_acc[(b, h)][:], func=ACT.Copy, scale=inv_sum[b][:])
+                nc.scalar.activation(out=result[:], in_=out_acc[(b, h)][:], func=ACT.Copy, scale=inv_sum[:, b : b + 1])
             nc.sync.dma_start(out=out[b][:, channels], in_=result[:])
 
         def busy_passes(n):
@@ -312,13 +310,13 @@ def tile_probcrossattention_pb_s_kernel(tc, q, k_mu, k_var, v_sample, out):
             )
         for b in range(B):
             scores(b)
-        for n in (1, 1, 1, 2):
+        for n in (1, 1, 2, 2):
             busy_passes(n)
         for b in range(B):
             scores_min(b)
             e_exp(b)
             e_transposes(b)
-        busy_passes(2)
+        busy_passes(3)
         v_regroup(on_scalar, 1, 3 * QUARTER, C)
         for b in range(B):
             e_copy(b)
@@ -326,8 +324,7 @@ def tile_probcrossattention_pb_s_kernel(tc, q, k_mu, k_var, v_sample, out):
         v_regroup(on_vector, 1, 0, 3 * QUARTER)
         for b in range(B):
             v_quantise(b)
-        for b in range(B):
-            nc.vector.reciprocal(out=inv_sum[b][:], in_=row_sum[b][:])
+        nc.vector.reciprocal(out=inv_sum[:], in_=row_sum[:])
         for b in range(B):
             e_quantise(b)
             for h in range(2):

@@ -47,10 +47,9 @@ def tile_probcrossattention_pb_s_kernel(tc, q, k_mu, k_var, v_sample, out):
         def sbuf(shape, dtype, name):
             return keep.tile(shape, dtype, name=name, align_bytes=64)
 
-        q_raw = sbuf([P, B * C], BF16, "q_raw")
-        nc.sync.dma_start(
-            out=q_raw[:].rearrange("p (b c) -> p b c", b=B), in_=q.rearrange("b q c -> q b c")
-        )
+        q_raw = [sbuf([P, C], BF16, "q_raw%d" % b) for b in range(B)]
+        for b in range(B):
+            nc.sync.dma_start(out=q_raw[b][:], in_=q[b])
         k_dram = {"var": k_var, "mu": k_mu}
         k_raw = {}
         for x in K_ORDER:
@@ -126,21 +125,23 @@ def tile_probcrossattention_pb_s_kernel(tc, q, k_mu, k_var, v_sample, out):
         k_acc = {}
         out_acc = {}
 
-        def q_transposes():
-            banks["q"] = psum_tr.tile([P, B, 2, P], F32, name="q_bank", tag="bank")
-            words = q_raw[:].bitcast(F32).rearrange("p (b u w) -> p b u w", b=B, u=2)
-            for b in range(B):
-                for u in range(2):
-                    nc.tensor.transpose(banks["q"][:, b, u, :], words[:, b, u, :], ident_f32[:])
+        def q_transposes(b):
+            banks[b] = psum_tr.tile([P, 2, P], F32, name="q_bank", tag="bank")
+            words = q_raw[b][:].bitcast(F32).rearrange("p (u w) -> p u w", u=2)
+            for u in range(2):
+                nc.tensor.transpose(banks[b][:, u, :], words[:, u, :], ident_f32[:])
 
-        def q_copy(copy):
+        def q_copy(copy, b):
             copy(
-                out=q_grouped[:].bitcast(F32).rearrange("p (b r u) -> p b r u", b=B, u=2),
-                in_=banks["q"][:].rearrange("p b u r -> p b r u"),
+                out=q_grouped[:].bitcast(F32).rearrange("p (b r u) -> p b r u", b=B, u=2)[:, b],
+                in_=banks[b][:].rearrange("p u r -> p r u"),
             )
 
-        def q_square():
-            nc.vector.tensor_tensor(out=q2_grouped[:], in0=q_grouped[:], in1=q_grouped[:], op=ALU.mult)
+        def q_square(b):
+            cols = slice(b * TQ * PACK, (b + 1) * TQ * PACK)
+            nc.vector.tensor_tensor(
+                out=q2_grouped[:, cols], in0=q_grouped[:, cols], in1=q_grouped[:, cols], op=ALU.mult
+            )
 
         def q_quantise(kind):
             nc.vector.quantize_mx(
@@ -271,9 +272,11 @@ def tile_probcrossattention_pb_s_kernel(tc, q, k_mu, k_var, v_sample, out):
         on_vector = nc.vector.tensor_copy
         var0, var1, mu0, mu1 = K_ORDER
 
-        q_transposes()
-        q_copy(on_scalar)
-        q_square()
+        for b in range(B):
+            q_transposes(b)
+            q_copy(on_scalar, b)
+        for b in range(B):
+            q_square(b)
         q_quantise("mu")
         q_quantise("var")
 
@@ -297,17 +300,14 @@ def tile_probcrossattention_pb_s_kernel(tc, q, k_mu, k_var, v_sample, out):
 
         gate = sbuf([P, 1], F32, "gate")
         nc.vector.memset(gate[:], 1.0)
-        for i in range(3):
-            nc.gpsimd.tensor_scalar(
-                out=v_grouped[0][:, i * QUARTER * PACK : (i + 1) * QUARTER * PACK].rearrange(
-                    "p (c t) -> p c t", t=PACK
-                ),
-                in0=v_raw[0][:].rearrange("p (t c) -> p c t", t=PACK)[:, i * QUARTER : (i + 1) * QUARTER],
-                scalar1=gate[:],
-                scalar2=0.0,
-                op0=ALU.mult,
-                op1=ALU.add,
-            )
+        nc.gpsimd.tensor_scalar(
+            out=v_grouped[0][:].rearrange("p (c t) -> p c t", t=PACK),
+            in0=v_raw[0][:].rearrange("p (t c) -> p c t", t=PACK),
+            scalar1=gate[:],
+            scalar2=0.0,
+            op0=ALU.mult,
+            op1=ALU.add,
+        )
         for b in range(B):
             scores(b)
         for n in (1, 1, 2, 2):
@@ -317,11 +317,9 @@ def tile_probcrossattention_pb_s_kernel(tc, q, k_mu, k_var, v_sample, out):
             e_exp(b)
             e_transposes(b)
         busy_passes(3)
-        v_regroup(on_scalar, 1, 3 * QUARTER, C)
         for b in range(B):
             e_copy(b)
-        v_regroup(on_vector, 0, 3 * QUARTER, C)
-        v_regroup(on_vector, 1, 0, 3 * QUARTER)
+        v_regroup(on_vector, 1, 0, C)
         for b in range(B):
             v_quantise(b)
         nc.vector.reciprocal(out=inv_sum[:], in_=row_sum[:])

@@ -169,16 +169,19 @@ def tile_probcrossattention_pb_s_kernel(tc, q, k_mu, k_var, v_sample, out):
                 in_=k_grouped[x][:, h * HALF * PACK : (h + 1) * HALF * PACK],
             )
 
-        def k_matmul(x):
+        def k_matmul(x, parts=1):
             kind, b = x
             k_acc[x] = psum_acc.tile([P, TK], F32, name="k_acc", tag="acc")
             queries = slice(b * TQ, (b + 1) * TQ)
-            mx_pass(
-                nc,
-                k_acc[x][:],
-                (q_codes[kind][:, queries], q_scales[kind][:, queries]),
-                (k_codes[x][:], k_scales[x][:]),
-            )
+            width = TK // parts
+            for i in range(parts):
+                keys = slice(i * width, (i + 1) * width)
+                mx_pass(
+                    nc,
+                    k_acc[x][:, keys],
+                    (q_codes[kind][:, queries], q_scales[kind][:, queries]),
+                    (k_codes[x][:, keys], k_scales[x][:, keys]),
+                )
 
         def penalty_sqrt(b):
             nc.scalar.activation(
@@ -274,7 +277,7 @@ def tile_probcrossattention_pb_s_kernel(tc, q, k_mu, k_var, v_sample, out):
 
         for b in range(B):
             q_transposes(b)
-            q_copy(on_scalar, b)
+            q_copy((on_scalar, on_vector)[b], b)
         for b in range(B):
             q_square(b)
         q_quantise("mu")
@@ -291,8 +294,9 @@ def tile_probcrossattention_pb_s_kernel(tc, q, k_mu, k_var, v_sample, out):
         k_copy(on_vector, mu1, 1)
         for h in range(2):
             k_quantise(mu1, h)
-        for x in K_ORDER:
+        for x in (var0, var1, mu0):
             k_matmul(x)
+        k_matmul(mu1, parts=2)
         for b in range(B):
             penalty_sqrt(b)
         warm_exp = sbuf([P, 1], F32, "warm_exp")

import math
from contextlib import ExitStack

import concourse.mybir as mybir
from concourse.masks import make_identity

BF16 = mybir.dt.bfloat16
F32 = mybir.dt.float32
U32 = mybir.dt.uint32
U8 = mybir.dt.uint8
FP8X4 = mybir.dt.float8_e4m3fn_x4
ACT = mybir.ActivationFunctionType
ALU = mybir.AluOpType
AX = mybir.AxisListType

B, TQ, TK, C = 2, 128, 512, 512
BETA = 2.35
P = 128
PACK = 4
FLOPS = 3 * 2 * B * TQ * TK * C

K_ORDER = (("var", 0), ("var", 1), ("mu", 0), ("mu", 1))
HALF = 256
QUARTER = 128


def mx_pass(nc, acc, stationary, moving):
    nc.tensor.matmul_mx(
        out=acc,
        lhsT=stationary[0].bitcast(FP8X4),
        lhsT_scale=stationary[1],
        rhs=moving[0].bitcast(FP8X4),
        rhs_scale=moving[1],
        start=True,
        stop=True,
    )


def tile_probcrossattention_pb_s_kernel(tc, q, k_mu, k_var, v_sample, out):
    nc = tc.nc
    with ExitStack() as ctx:
        keep = ctx.enter_context(tc.tile_pool(name="keep", bufs=1))
        psum_tr = ctx.enter_context(tc.psum_pool(name="psum_tr", bufs=4))
        psum_acc = ctx.enter_context(tc.psum_pool(name="psum_acc", bufs=4))
        ctx.enter_context(tc.manual_schedule())

        def sbuf(shape, dtype, name):
            return keep.tile(shape, dtype, name=name, align_bytes=64)

        q_raw = [sbuf([P, C], BF16, "q_raw%d" % b) for b in range(B)]
        for b in range(B):
            nc.sync.dma_start(out=q_raw[b][:], in_=q[b])
        k_dram = {"var": k_var, "mu": k_mu}
        k_raw = {}
        for x in K_ORDER:
            k_raw[x] = sbuf([P, PACK * C], BF16, "%s_raw%d" % x)
            for h in range(2):
                cols = slice(h * 2 * C, (h + 1) * 2 * C)
                nc.sync.dma_start(
                    out=k_raw[x][:, cols],
                    in_=k_dram[x[0]][x[1]].rearrange("(p j) c -> p (j c)", j=PACK)[:, cols],
                )
        v_raw = {}
        for b in range(B):
            v_raw[b] = sbuf([P, PACK * C], BF16, "v_raw%d" % b)
            nc.sync.dma_start(out=v_raw[b][:], in_=v_sample[b].rearrange("(p j) c -> p (j c)", j=PACK))

        zeros = sbuf([P, TK], BF16, "zeros")
        nc.vector.memset(zeros[:], 0.0)
        zero_codes = sbuf([P, TK // PACK], U32, "zero_codes")
        zero_scales = sbuf([P, TK // PACK], U8, "zero_scales")
        nc.vector.quantize_mx(out=zero_codes[:].bitcast(FP8X4), scales=zero_scales[:], in_=zeros[:])
        warm = psum_acc.tile([P, TK], F32, name="warm", tag="acc")
        for i in range(2):
            nc.tensor.matmul(warm[:], lhsT=zeros[:, 0:P], rhs=zeros[:], start=True, stop=True)
        for i in range(6):
            mx_pass(nc, warm[:, 0:P], (zero_codes[:], zero_scales[:]), (zero_codes[:], zero_scales[:]))

        ident_f32 = sbuf([P, P], F32, "ident_f32")
        make_identity(nc, ident_f32[:])
        one = sbuf([P, 1], F32, "one")
        nc.vector.memset(one[:], 1.0)
        warm_sqrt = sbuf([P, 1], F32, "warm_sqrt")
        nc.scalar.activation(out=warm_sqrt[:], in_=one[:], func=ACT.Sqrt)

        q_grouped = sbuf([P, B * TQ * PACK], BF16, "q_grouped")
        q2_grouped = sbuf([P, B * TQ * PACK], BF16, "q2_grouped")
        q_grouped_of = {"mu": q_grouped, "var": q2_grouped}
        q_codes = {}
        q_scales = {}
        for kind in ("mu", "var"):
            q_codes[kind] = sbuf([P, B * TQ], U32, "q_codes_" + kind)
            q_scales[kind] = sbuf([P, B * TQ], U8, "q_scales_" + kind)
        k_grouped = {}
        k_codes = {}
        k_scales = {}
        for x in K_ORDER:
            k_grouped[x] = sbuf([P, TK * PACK], BF16, "%s_grouped%d" % x)
            k_codes[x] = sbuf([P, TK], U32, "%s_codes%d" % x)
            k_scales[x] = sbuf([P, TK], U8, "%s_scales%d" % x)
        v_grouped = {}
        v_codes = {}
        v_scales = {}
        e_bf16 = {}
        e_grouped = {}
        e_codes = {}
        e_scales = {}
        penalty = {}
        neg_scores = {}
        neg_max = {}
        row_sum = sbuf([P, B], F32, "row_sum")
        inv_sum = sbuf([P, B], F32, "inv_sum")
        for b in range(B):
            v_grouped[b] = sbuf([P, C * PACK], BF16, "v_grouped%d" % b)
            v_codes[b] = sbuf([P, C], U32, "v_codes%d" % b)
            v_scales[b] = sbuf([P, C], U8, "v_scales%d" % b)
            e_bf16[b] = sbuf([P, TK], BF16, "e_bf16_%d" % b)
            e_grouped[b] = sbuf([P, TQ * PACK], BF16, "e_grouped%d" % b)
            e_codes[b] = sbuf([P, TQ], U32, "e_codes%d" % b)
            e_scales[b] = sbuf([P, TQ], U8, "e_scales%d" % b)
            penalty[b] = sbuf([P, TK], F32, "penalty%d" % b)
            neg_scores[b] = sbuf([P, TK], F32, "neg_scores%d" % b)
            neg_max[b] = sbuf([P, 1], F32, "neg_max%d" % b)
        banks = {}
        k_acc = {}
        out_acc = {}

        def q_transposes(b):
            banks[b] = psum_tr.tile([P, 2, P], F32, name="q_bank", tag="bank")
            words = q_raw[b][:].bitcast(F32).rearrange("p (u w) -> p u w", u=2)
            for u in range(2):
                nc.tensor.transpose(banks[b][:, u, :], words[:, u, :], ident_f32[:])

        def q_copy(copy, b):
            copy(
                out=q_grouped[:].bitcast(F32).rearrange("p (b r u) -> p b r u", b=B, u=2)[:, b],
                in_=banks[b][:].rearrange("p u r -> p r u"),
            )

        def q_square(b):
            cols = slice(b * TQ * PACK, (b + 1) * TQ * PACK)
            nc.vector.tensor_tensor(
                out=q2_grouped[:, cols], in0=q_grouped[:, cols], in1=q_grouped[:, cols], op=ALU.mult
            )

        def q_quantise(kind):
            nc.vector.quantize_mx(
                out=q_codes[kind][:].bitcast(FP8X4), scales=q_scales[kind][:], in_=q_grouped_of[kind][:]
            )

        def k_transposes(x, h):
            banks[x + (h,)] = psum_tr.tile([P, 2, 2, P], F32, name="bank", tag="bank")
            words = k_raw[x][:].bitcast(F32).rearrange("p (h j u w) -> p h j u w", h=2, j=2, u=2)
            for j in range(2):
                for u in range(2):
                    nc.tensor.transpose(banks[x + (h,)][:, j, u, :], words[:, h, j, u, :], ident_f32[:])

        def k_copy(copy, x, h):
            copy(
                out=k_grouped[x][:].bitcast(F32).rearrange("p (h r j u) -> p h r j u", h=2, j=2, u=2)[:, h],
                in_=banks[x + (h,)][:].rearrange("p j u r -> p r j u"),
            )

        def k_quantise(x, h):
            keys = slice(h * HALF, (h + 1) * HALF)
            nc.vector.quantize_mx(
                out=k_codes[x][:, keys].bitcast(FP8X4),
                scales=k_scales[x][:, keys],
                in_=k_grouped[x][:, h * HALF * PACK : (h + 1) * HALF * PACK],
            )

        def k_matmul(x, parts=1):
            kind, b = x
            k_acc[x] = psum_acc.tile([P, TK], F32, name="k_acc", tag="acc")
            queries = slice(b * TQ, (b + 1) * TQ)
            width = TK // parts
            for i in range(parts):
                keys = slice(i * width, (i + 1) * width)
                mx_pass(
                    nc,
                    k_acc[x][:, keys],
                    (q_codes[kind][:, queries], q_scales[kind][:, queries]),
                    (k_codes[x][:, keys], k_scales[x][:, keys]),
                )

        def penalty_sqrt(b):
            nc.scalar.activation(
                out=penalty[b][:], in_=k_acc[("var", b)][:], func=ACT.Sqrt, scale=BETA * BETA / C
            )

        def scores(b):
            nc.vector.scalar_tensor_tensor(
                out=neg_scores[b][:],
                in0=k_acc[("mu", b)][:],
                scalar=-1.0 / math.sqrt(C),
                in1=penalty[b][:],
                op0=ALU.mult,
                op1=ALU.add,
            )

        def scores_min(b):
            nc.vector.tensor_reduce(out=neg_max[b][:], in_=neg_scores[b][:], axis=AX.X, op=ALU.min)

        def v_regroup(copy, b, c0, c1):
            copy(
                out=v_grouped[b][:, c0 * PACK : c1 * PACK].rearrange("p (c i t) -> p c t i", i=4, t=PACK),
                in_=v_raw[b][:].rearrange("p (t c i) -> p c t i", t=PACK, i=4)[:, c0 // 4 : c1 // 4],
            )

        def v_quantise(b):
            nc.vector.quantize_mx(
                out=v_codes[b][:].bitcast(FP8X4), scales=v_scales[b][:], in_=v_grouped[b][:]
            )

        def e_exp(b):
            nc.scalar.activation(
                out=e_bf16[b][:],
                in_=neg_scores[b][:],
                func=ACT.Exp,
                bias=neg_max[b][:],
                scale=-1.0,
                accum_out=row_sum[:, b : b + 1],
            )

        def e_transposes(b):
            banks[("e", b)] = psum_tr.tile([P, 2, TQ], F32, name="e_t", tag="bank")
            for u in range(2):
                nc.tensor.transpose(
                    banks[("e", b)][:, u, :],
                    e_bf16[b][:].bitcast(F32)[:, u * P : (u + 1) * P],
                    ident_f32[:],
                )

        def e_copy(b):
            nc.scalar.copy(
                out=e_grouped[b][:].bitcast(F32).rearrange("p (r u) -> p r u", u=2),
                in_=banks[("e", b)][:].rearrange("p u r -> p r u"),
            )

        def e_quantise(b):
            nc.vector.quantize_mx(
                out=e_codes[b][:].bitcast(FP8X4), scales=e_scales[b][:], in_=e_grouped[b][:]
            )

        def out_matmul(b, h):
            channels = slice(h * HALF, (h + 1) * HALF)
            out_acc[(b, h)] = psum_acc.tile([P, HALF], F32, name="out_acc", tag="acc")
            mx_pass(
                nc,
                out_acc[(b, h)][:],
                (e_codes[b][:], e_scales[b][:]),
                (v_codes[b][:, channels], v_scales[b][:, channels]),
            )

        def out_store(on_vector, b, h):
            channels = slice(h * HALF, (h + 1) * HALF)
            result = sbuf([P, HALF], F32, "out%d_%d" % (b, h))
            if on_vector:
                nc.vector.tensor_scalar_mul(out=result[:], in0=out_acc[(b, h)][:], scalar1=inv_sum[:, b : b + 1])
            else:
                nc.scalar.activation(out=result[:], in_=out_acc[(b, h)][:], func=ACT.Copy, scale=inv_sum[:, b : b + 1])
            nc.sync.dma_start(out=out[b][:, channels], in_=result[:])

        def busy_passes(n):
            again = psum_acc.tile([P, TK], F32, name="again", tag="acc")
            for i in range(n):
                mx_pass(
                    nc,
                    again[:],
                    (q_codes["var"][:, 0:TQ], q_scales["var"][:, 0:TQ]),
                    (k_codes[("var", 0)][:], k_scales[("var", 0)][:]),
                )

        on_scalar = nc.scalar.copy
        on_vector = nc.vector.tensor_copy
        var0, var1, mu0, mu1 = K_ORDER

        for b in range(B):
            q_transposes(b)
            q_copy((on_scalar, on_vector)[b], b)
        for b in range(B):
            q_square(b)
        q_quantise("mu")
        q_quantise("var")

        for x in (var0, var1, mu0):
            for h in range(2):
                k_transposes(x, h)
                k_copy(on_scalar, x, h)
                k_quantise(x, h)
        for h in range(2):
            k_transposes(mu1, h)
        k_copy(on_scalar, mu1, 0)
        k_copy(on_vector, mu1, 1)
        for h in range(2):
            k_quantise(mu1, h)
        for x in (var0, var1, mu0):
            k_matmul(x)
        k_matmul(mu1, parts=2)
        for b in range(B):
            penalty_sqrt(b)
        warm_exp = sbuf([P, 1], F32, "warm_exp")
        nc.scalar.activation(out=warm_exp[:], in_=one[:], func=ACT.Exp)

        gate = sbuf([P, 1], F32, "gate")
        nc.vector.memset(gate[:], 1.0)
        nc.gpsimd.tensor_scalar(
            out=v_grouped[0][:].rearrange("p (c t) -> p c t", t=PACK),
            in0=v_raw[0][:].rearrange("p (t c) -> p c t", t=PACK),
            scalar1=gate[:],
            scalar2=0.0,
            op0=ALU.mult,
            op1=ALU.add,
        )
        for b in range(B):
            scores(b)
        for n in (1, 1, 2, 2):
            busy_passes(n)
        for b in range(B):
            scores_min(b)
            e_exp(b)
            e_transposes(b)
        busy_passes(3)
        for b in range(B):
            e_copy(b)
        v_regroup(on_vector, 1, 0, C)
        for b in range(B):
            v_quantise(b)
        nc.vector.reciprocal(out=inv_sum[:], in_=row_sum[:])
        for b in range(B):
            e_quantise(b)
            for h in range(2):
                out_matmul(b, h)
        for b in range(B):
            for h in range(2):
                out_store(h == 1, b, h)
